import numpy as np
import ml_dtypes


def mxq(x, axis, fmt="e4m3"):
    dtype, down = {"e4m3": (ml_dtypes.float8_e4m3fn, 7), "e5m2": (ml_dtypes.float8_e5m2, 14)}[fmt]
    v = np.moveaxis(np.asarray(x, np.float32).astype(ml_dtypes.bfloat16).astype(np.float64), axis, -1)
    blocks = v.reshape(v.shape[:-1] + (-1, 32))
    amax = np.abs(blocks).max(-1, keepdims=True)
    byte = np.maximum(np.where(amax > 0, np.frexp(amax)[1] - 1 + 127, 0) - down, 1)
    scale = np.exp2(byte - 127.0)
    codes = (blocks / scale).astype(np.float32).astype(dtype).astype(np.float64)
    return np.moveaxis((codes * scale).reshape(v.shape), -1, axis)


WIDE = False


def mx_kscale(k):
    if not WIDE:
        return np.ones(k)
    levels = np.array([10, -10, 5, -5, 0])
    if k % 512:
        return np.exp2(np.random.permutation(np.resize(levels, k // 32))).repeat(32)
    a = np.empty((k // 512, 16))
    for p in range(k // 512):
        a[p, :8] = np.random.permutation(np.resize(levels, 8))
        for g in range(8):
            far = levels[np.abs(levels - a[p, g]) >= 10]
            a[p, g + 8] = far[np.random.randint(len(far))]
    return np.exp2(a.ravel()).repeat(32)


BF16 = ml_dtypes.bfloat16


def bf(x):
    return np.asarray(x, np.float32).astype(BF16)


def f64(x):
    return np.asarray(x).astype(np.float64)


H, D, L = 4, 512, 1024
HD = H * D


def split_heads(x):
    return x.reshape(L, H, D).transpose(1, 2, 0)


def setup_inputs():
    s, t = mx_kscale(D), mx_kscale(L)
    tr = np.repeat(t, HD // L)
    e = np.exp(1.5 * np.random.standard_normal((H, L, L)))
    return {"attn": bf(e / e.sum(0, keepdims=True) / t),
            "tokens": bf(np.random.standard_normal((D, L)) * s[:, None]),
            "Wv": bf(np.random.standard_normal((HD, D)) * 0.5 / np.sqrt(D) / s * tr[:, None]),
            "bv": bf(np.random.standard_normal(HD) * 0.15 * tr)}


def reference(attn, tokens, Wv, bv):
    v = split_heads((mxq(f64(Wv), 1, "e4m3") @ mxq(f64(tokens), 0, "e4m3")) + f64(bv)[:, None])
    return mxq(v, 2, "e4m3") @ mxq(f64(attn).transpose(0, 2, 1), 1, "e4m3")

@@ -1,0 +1,271 @@
+from contextlib import ExitStack
+
+import concourse.mybir as mybir
+from concourse.masks import make_identity
+
+F32 = mybir.dt.float32
+BF16 = mybir.dt.bfloat16
+U32 = mybir.dt.uint32
+U8 = mybir.dt.uint8
+FP8X4 = mybir.dt.float8_e4m3fn_x4
+ADD = mybir.AluOpType.add
+
+P = 128
+FLOPS = 2 * 2048 * 1024 * 512 + 2 * 4 * 512 * 1024 * 1024
+
+PIN = True
+LEAD = 8
+FIRST_LOADS = 4
+
+
+def tile_selfattention_pb_t_kernel(tc, attn, tokens, Wv, bv, out):
+    nc = tc.nc
+    with ExitStack() as ctx:
+        const = ctx.enter_context(tc.tile_pool(name="const", bufs=1))
+        raw = ctx.enter_context(tc.tile_pool(name="raw", bufs=1))
+        codes = ctx.enter_context(tc.tile_pool(name="codes", bufs=1))
+        sgrp = ctx.enter_context(tc.tile_pool(name="sgrp", bufs=5))
+        wgrp = ctx.enter_context(tc.tile_pool(name="wgrp", bufs=4))
+        tgrp = ctx.enter_context(tc.tile_pool(name="tgrp", bufs=2))
+        vgrp = ctx.enter_context(tc.tile_pool(name="vgrp", bufs=4))
+        outp = ctx.enter_context(tc.tile_pool(name="outp", bufs=8))
+        psum = ctx.enter_context(tc.psum_pool(name="psum", bufs=8))
+        if PIN:
+            ctx.enter_context(tc.manual_schedule())
+
+        wv_view = Wv.rearrange("(g q u e a) k -> g u a q e k", g=2, u=2, e=2, a=2)
+        tok_view = tokens.rearrange("(q t) c -> q t c", t=4)
+        wv_raw = {
+            (a, gu): raw.tile([P, 2, 512], BF16, name="wv_raw%d%d" % (a, gu)) for a in range(2) for gu in range(4)
+        }
+        tok_raw = [raw.tile([P, 4, 512], BF16, name="tok_raw%d" % cb) for cb in range(2)]
+        at_raw = {(i, j): raw.tile([P, 2048], BF16, name="at_raw%d%d" % (i, j)) for i in range(8) for j in range(2)}
+        bias_raw = const.tile([P, 2, 4, 2], BF16, name="bias_raw")
+        bias_f = const.tile([P, 2, 8], F32, name="bias_f")
+        ident = const.tile([P, P], F32, name="ident")
+
+        def load_attn(i):
+            h, lh = divmod(i, 2)
+            view = attn[h, lh * 512 : (lh + 1) * 512, :].rearrange("(lp j b) m -> j lp (b m)", j=2, b=2)
+            for j in (0, 1):
+                nc.sync.dma_start(out=at_raw[(i, j)][:], in_=view[j])
+
+        def load_wv(a, g):
+            for u in (0, 1):
+                nc.sync.dma_start(out=wv_raw[(a, 2 * g + u)][:], in_=wv_view[g, u, a])
+
+        with nc.allow_non_contiguous_dma(reason="bias: 8-byte runs, 4 KiB in all"):
+            nc.scalar.dma_start(
+                out=bias_raw[:], in_=bv.rearrange("(g q t a) -> q g t a", g=2, t=4, a=2)
+            )
+        make_identity(nc, ident[:])
+        def load_tokens(cb):
+            for u in (0, 1):
+                nc.sync.dma_start(
+                    out=tok_raw[cb][:, 2 * u : 2 * u + 2, :],
+                    in_=tok_view[:, 2 * u : 2 * u + 2, cb * 512 : (cb + 1) * 512],
+                )
+
+        load_wv(0, 0)
+        load_tokens(0)
+        load_wv(0, 1)
+        load_attn(0)
+        load_tokens(1)
+        load_attn(1)
+        load_wv(1, 0)
+        load_wv(1, 1)
+        for i in range(2, FIRST_LOADS):
+            load_attn(i)
+
+        def code_pair(name, width):
+            c = codes.tile([P, width], U32, name=name + "_c", align_bytes=64)
+            s = codes.tile([P, width], U8, name=name + "_s", align_bytes=64)
+            return c, s
+
+        tok_cs = [code_pair("tok%d" % cb, 512) for cb in range(2)]
+        wv_cs = {(a, g): code_pair("wv%d%d" % (a, g), 512) for a in range(2) for g in range(2)}
+        at_cs = {(i, g): code_pair("at%d%d" % (i, g), 512) for i in range(8) for g in range(2)}
+        v_cs = {
+            (h, g, k): code_pair("v%d%d%d" % (h, g, k), P)
+            for h in range(4)
+            for g in range(2)
+            for k in range(4)
+        }
+
+        def quantise(pair, grp):
+            nc.vector.quantize_mx(out=pair[0][:].bitcast(FP8X4), scales=pair[1][:], in_=grp[:])
+
+        live = {"waiting": None}
+
+        def new_bank():
+            bank = psum.tile([P, 512], F32, name="bank", tag="bank")
+            return bank
+
+        def copy_out(eng, dst, src):
+            if eng == "s":
+                nc.scalar.copy(out=dst, in_=src)
+            else:
+                nc.vector.tensor_copy(out=dst, in_=src)
+
+        def transposes(key, words, offs):
+            bank = new_bank()
+            for n, off in enumerate(offs):
+                nc.tensor.transpose(bank[:, n * P : (n + 1) * P], words[:, off : off + 2 * P - 1 : 2], ident[:])
+            live[key] = bank
+
+        def evac_words(key, grp, half, eng):
+            dst = grp[:].bitcast(F32)[:, half * 512 : (half + 1) * 512].rearrange(
+                "p (b c k) -> p b c k", b=2, k=2
+            )
+            copy_out(eng, dst, live[key][:].rearrange("p (b k c) -> p b c k", b=2, k=2))
+
+        def wt(a, g, u, eng="s"):
+            words = wv_raw[(a, 2 * g + u)][:].rearrange("q e k -> q (e k)").bitcast(F32)
+            transposes(("wt", a, g, u), words, [e * 256 + uk for e in (0, 1) for uk in (0, 1)])
+            if u == 0:
+                live[("wg", a, g)] = wgrp.tile([P, 2048], BF16, name="grp_w", tag="w", align_bytes=64)
+            evac_words(("wt", a, g, u), live[("wg", a, g)], u, eng)
+
+        def wq(a, g):
+            quantise(wv_cs[(a, g)], live[("wg", a, g)])
+
+        def tk_r(cb, eng):
+            tg = tgrp.tile([P, 2048], BF16, name="grp_t", tag="t", align_bytes=64)
+            copy_out(
+                eng,
+                tg[:].rearrange("p (c i t) -> p c t i", i=4, t=4),
+                tok_raw[cb][:].rearrange("p t (c i) -> p c t i", i=4),
+            )
+            live[("tg", cb)] = tg
+
+        def tk_q(cb):
+            quantise(tok_cs[cb], live[("tg", cb)])
+
+        def m1(n):
+            h, g, k = n // 8, (n // 4) % 2, n % 4
+            a, cb = divmod(h, 2)
+            bank = new_bank()
+            wc, ws = wv_cs[(a, g)]
+            tcd, tsc = tok_cs[cb]
+            for t in range(4):
+                nc.tensor.matmul_mx(
+                    out=bank[:, t * P : (t + 1) * P],
+                    lhsT=wc[:, t * P : (t + 1) * P].bitcast(FP8X4),
+                    lhsT_scale=ws[:, t * P : (t + 1) * P],
+                    rhs=tcd[:, k * P : (k + 1) * P].bitcast(FP8X4),
+                    rhs_scale=tsc[:, k * P : (k + 1) * P],
+                    start=True,
+                    stop=True,
+                )
+            live[("vb", n)] = bank
+
+        def ve(n):
+            h, g, k = n // 8, (n // 4) % 2, n % 4
+            vg = vgrp.tile([P, 512], BF16, name="grp_v", tag="v", align_bytes=64)
+            nc.vector.tensor_tensor(
+                out=vg[:].rearrange("q (d t) -> q d t", t=4),
+                in0=live[("vb", n)][:].rearrange("q (t d) -> q d t", t=4),
+                in1=bias_f[:, h // 2, 4 * g : 4 * g + 4].unsqueeze(1).to_broadcast([P, P, 4]),
+                op=ADD,
+            )
+            vq_flush()
+            live["waiting"] = (v_cs[(h, g, k)], vg)
+
+        def vq_flush():
+            if live["waiting"] is not None:
+                quantise(live["waiting"][0], live["waiting"][1])
+            live["waiting"] = None
+
+        def at(i, halves=(0, 1)):
+            if 0 in halves:
+                for g in (0, 1):
+                    live[("ag", i, g)] = sgrp.tile([P, 2048], BF16, name="grp_s", tag="s", align_bytes=64)
+            for j in halves:
+                words = at_raw[(i, j)][:].bitcast(F32)
+                for g in (0, 1):
+                    transposes(
+                        ("at", i, g, j),
+                        words,
+                        [b * 512 + g * 256 + u for b in (0, 1) for u in (0, 1)],
+                    )
+                    evac_words(("at", i, g, j), live[("ag", i, g)], j, "s")
+
+        def aq(i, g):
+            quantise(at_cs[(i, g)], live[("ag", i, g)])
+
+        def m2(j, eng):
+            h, lh, k = j // 8, (j // 4) % 2, j % 4
+            bank = new_bank()
+            for g in (0, 1):
+                vc, vs = v_cs[(h, g, k)]
+                ac, asc = at_cs[(2 * h + lh, g)]
+                nc.tensor.matmul_mx(
+                    out=bank[:],
+                    lhsT=vc[:].bitcast(FP8X4),
+                    lhsT_scale=vs[:],
+                    rhs=ac[:].bitcast(FP8X4),
+                    rhs_scale=asc[:],
+                    start=(g == 0),
+                    stop=(g == 1),
+                )
+            osb = outp.tile([P, 512], F32, name="out_sb", tag="o")
+            copy_out(
+                eng,
+                osb[:].rearrange("d (lp lb) -> d lp lb", lb=4),
+                bank[:].rearrange("d (lb lp) -> d lp lb", lb=4),
+            )
+            nc.sync.dma_start(out=out[h, k * P : (k + 1) * P, lh * 512 : (lh + 1) * 512], in_=osb[:])
+
+        for g in (0, 1):
+            for u in (0, 1):
+                wt(0, g, u)
+        tk_r(0, "v")
+        wq(0, 0)
+        tk_q(0)
+        for n in range(4):
+            m1(n)
+        for a in (0, 1):
+            nc.vector.tensor_copy(
+                out=bias_f[:, a, :].rearrange("q (g t) -> q g t", t=4), in_=bias_raw[:, :, :, a]
+            )
+        ve(0)
+        ve(1)
+        wq(0, 1)
+        ve(2)
+        ve(3)
+        tk_r(1, "v")
+        at(0)
+        for n in range(4, LEAD):
+            m1(n)
+            ve(n)
+        aq(0, 0)
+        tk_q(1)
+        aq(0, 1)
+        at(1)
+        for g in (0, 1):
+            for u in (0, 1):
+                wt(1, g, u)
+        for p in range(8):
+            if p + 2 < 8:
+                at(p + 2, (0,))
+            if p + 1 < 8:
+                aq(p + 1, 0)
+            for k in range(4):
+                if k == 2 and p + 2 < 8:
+                    at(p + 2, (1,))
+                if k == 2 and p + 1 < 8:
+                    aq(p + 1, 1)
+                j = 4 * p + k
+                n = j + LEAD
+                m2(j, "v" if (n >= 32 and j % 2 == 1) else "s")
+                if n < 32:
+                    m1(n)
+                    ve(n)
+                if n == 31:
+                    vq_flush()
+                if p == 0 and k == 1:
+                    wq(1, 0)
+                if p == 0 and k == 3:
+                    wq(1, 1)
+            if p + FIRST_LOADS < 8:
+                load_attn(p + FIRST_LOADS)

@@ -13,7 +13,6 @@ ADD = mybir.AluOpType.add
 P = 128
 FLOPS = 2 * 2048 * 1024 * 512 + 2 * 4 * 512 * 1024 * 1024
 
-PIN = True
 LEAD = 8
 FIRST_LOADS = 4
 
@@ -30,8 +29,7 @@ def tile_selfattention_pb_t_kernel(tc, attn, tokens, Wv, bv, out):
         vgrp = ctx.enter_context(tc.tile_pool(name="vgrp", bufs=4))
         outp = ctx.enter_context(tc.tile_pool(name="outp", bufs=8))
         psum = ctx.enter_context(tc.psum_pool(name="psum", bufs=8))
-        if PIN:
-            ctx.enter_context(tc.manual_schedule())
+        ctx.enter_context(tc.manual_schedule())
 
         wv_view = Wv.rearrange("(g q u e a) k -> g u a q e k", g=2, u=2, e=2, a=2)
         tok_view = tokens.rearrange("(q t) c -> q t c", t=4)
@@ -257,12 +255,13 @@ def tile_selfattention_pb_t_kernel(tc, attn, tokens, Wv, bv, out):
                     aq(p + 1, 1)
                 j = 4 * p + k
                 n = j + LEAD
-                m2(j, "v" if (n >= 32 and j % 2 == 1) else "s")
-                if n < 32:
-                    m1(n)
-                    ve(n)
+                if n < 32 and k % 2 == 0:
+                    for i in (n, n + 1):
+                        m1(i)
+                        ve(i)
                 if n == 31:
                     vq_flush()
+                m2(j, "v" if (n >= 32 and j % 2 == 1) else "s")
                 if p == 0 and k == 1:
                     wq(1, 0)
                 if p == 0 and k == 3:

@@ -13,8 +13,8 @@ ADD = mybir.AluOpType.add
 P = 128
 FLOPS = 2 * 2048 * 1024 * 512 + 2 * 4 * 512 * 1024 * 1024
 
-LEAD = 8
-FIRST_LOADS = 4
+LEAD = 4
+FIRST_LOADS = 5
 
 
 def tile_selfattention_pb_t_kernel(tc, attn, tokens, Wv, bv, out):
@@ -27,7 +27,7 @@ def tile_selfattention_pb_t_kernel(tc, attn, tokens, Wv, bv, out):
         wgrp = ctx.enter_context(tc.tile_pool(name="wgrp", bufs=4))
         tgrp = ctx.enter_context(tc.tile_pool(name="tgrp", bufs=2))
         vgrp = ctx.enter_context(tc.tile_pool(name="vgrp", bufs=4))
-        outp = ctx.enter_context(tc.tile_pool(name="outp", bufs=8))
+        outp = ctx.enter_context(tc.tile_pool(name="outp", bufs=4))
         psum = ctx.enter_context(tc.psum_pool(name="psum", bufs=8))
         ctx.enter_context(tc.manual_schedule())
 
@@ -68,11 +68,13 @@ def tile_selfattention_pb_t_kernel(tc, attn, tokens, Wv, bv, out):
         load_tokens(0)
         load_wv(0, 1)
         load_attn(0)
-        load_tokens(1)
         load_attn(1)
+        load_attn(2)
+        load_tokens(1)
+        load_attn(3)
         load_wv(1, 0)
         load_wv(1, 1)
-        for i in range(2, FIRST_LOADS):
+        for i in range(4, FIRST_LOADS):
             load_attn(i)
 
         def code_pair(name, width):
@@ -140,7 +142,7 @@ def tile_selfattention_pb_t_kernel(tc, attn, tokens, Wv, bv, out):
             quantise(tok_cs[cb], live[("tg", cb)])
 
         def m1(n):
-            h, g, k = n // 8, (n // 4) % 2, n % 4
+            h, k, g = n // 8, (n // 2) % 4, n % 2
             a, cb = divmod(h, 2)
             bank = new_bank()
             wc, ws = wv_cs[(a, g)]
@@ -158,7 +160,7 @@ def tile_selfattention_pb_t_kernel(tc, attn, tokens, Wv, bv, out):
             live[("vb", n)] = bank
 
         def ve(n):
-            h, g, k = n // 8, (n // 4) % 2, n % 4
+            h, k, g = n // 8, (n // 2) % 4, n % 2
             vg = vgrp.tile([P, 512], BF16, name="grp_v", tag="v", align_bytes=64)
             nc.vector.tensor_tensor(
                 out=vg[:].rearrange("q (d t) -> q d t", t=4),
@@ -192,7 +194,7 @@ def tile_selfattention_pb_t_kernel(tc, attn, tokens, Wv, bv, out):
             quantise(at_cs[(i, g)], live[("ag", i, g)])
 
         def m2(j, eng):
-            h, lh, k = j // 8, (j // 4) % 2, j % 4
+            h, k, lh = j // 8, (j // 2) % 4, j % 2
             bank = new_bank()
             for g in (0, 1):
                 vc, vs = v_cs[(h, g, k)]
@@ -206,13 +208,19 @@ def tile_selfattention_pb_t_kernel(tc, attn, tokens, Wv, bv, out):
                     start=(g == 0),
                     stop=(g == 1),
                 )
-            osb = outp.tile([P, 512], F32, name="out_sb", tag="o")
+            if lh == 0:
+                live["osb"] = outp.tile([P, 1024], F32, name="out_sb", tag="o")
+            osb = live["osb"]
             copy_out(
                 eng,
-                osb[:].rearrange("d (lp lb) -> d lp lb", lb=4),
+                osb[:, lh * 512 : (lh + 1) * 512].rearrange("d (lp lb) -> d lp lb", lb=4),
                 bank[:].rearrange("d (lb lp) -> d lp lb", lb=4),
             )
-            nc.sync.dma_start(out=out[h, k * P : (k + 1) * P, lh * 512 : (lh + 1) * 512], in_=osb[:])
+            if j >= 30:
+                l0 = lh * 512
+                nc.sync.dma_start(out=out[h, k * P : (k + 1) * P, l0 : l0 + 512], in_=osb[:, l0 : l0 + 512])
+            elif lh == 1:
+                nc.sync.dma_start(out=out[h, k * P : (k + 1) * P, :], in_=osb[:])
 
         for g in (0, 1):
             for u in (0, 1):
@@ -220,51 +228,49 @@ def tile_selfattention_pb_t_kernel(tc, attn, tokens, Wv, bv, out):
         tk_r(0, "v")
         wq(0, 0)
         tk_q(0)
-        for n in range(4):
-            m1(n)
+        wq(0, 1)
         for a in (0, 1):
             nc.vector.tensor_copy(
                 out=bias_f[:, a, :].rearrange("q (g t) -> q g t", t=4), in_=bias_raw[:, :, :, a]
             )
-        ve(0)
-        ve(1)
-        wq(0, 1)
-        ve(2)
-        ve(3)
-        tk_r(1, "v")
-        at(0)
-        for n in range(4, LEAD):
+        at(0, (0,))
+        for n in range(LEAD):
             m1(n)
             ve(n)
+        at(0, (1,))
         aq(0, 0)
-        tk_q(1)
         aq(0, 1)
         at(1)
-        for g in (0, 1):
-            for u in (0, 1):
-                wt(1, g, u)
-        for p in range(8):
-            if p + 2 < 8:
-                at(p + 2, (0,))
-            if p + 1 < 8:
-                aq(p + 1, 0)
-            for k in range(4):
-                if k == 2 and p + 2 < 8:
-                    at(p + 2, (1,))
-                if k == 2 and p + 1 < 8:
-                    aq(p + 1, 1)
-                j = 4 * p + k
+        aq(1, 0)
+        aq(1, 1)
+        for s in range(16):
+            early = 4 if s == 0 else s + 5
+            if early < 16:
+                at(early // 2, (early % 2,))
+            if s == 0:
+                tk_r(1, "v")
+            if s == 1:
+                tk_q(1)
+            if s in (4, 5):
+                wq(1, s - 4)
+            split = s in (0, 2, 3)
+            for j in (2 * s, 2 * s + 1):
                 n = j + LEAD
-                if n < 32 and k % 2 == 0:
-                    for i in (n, n + 1):
-                        m1(i)
-                        ve(i)
+                if s % 2 == 1 and (s + 3) // 2 < 8:
+                    aq((s + 3) // 2, j % 2)
+                if split and j % 2 == 1:
+                    m2(j - 1, "s")
+                    if s == 0:
+                        at(2, (1,))
+                    else:
+                        for u in (0, 1):
+                            wt(1, s - 2, u)
+                if n < 32:
+                    m1(n)
+                    ve(n)
                 if n == 31:
                     vq_flush()
-                m2(j, "v" if (n >= 32 and j % 2 == 1) else "s")
-                if p == 0 and k == 1:
-                    wq(1, 0)
-                if p == 0 and k == 3:
-                    wq(1, 1)
-            if p + FIRST_LOADS < 8:
-                load_attn(p + FIRST_LOADS)
+            for j in ((2 * s + 1,) if split else (2 * s, 2 * s + 1)):
+                m2(j, "v" if (j + LEAD >= 32 and j % 2 == 1) else "s")
+            if s % 2 == 1 and s // 2 + FIRST_LOADS < 8:
+                load_attn(s // 2 + FIRST_LOADS)

@@ -28,6 +28,7 @@ def tile_selfattention_pb_t_kernel(tc, attn, tokens, Wv, bv, out):
         tgrp = ctx.enter_context(tc.tile_pool(name="tgrp", bufs=2))
         vgrp = ctx.enter_context(tc.tile_pool(name="vgrp", bufs=4))
         outp = ctx.enter_context(tc.tile_pool(name="outp", bufs=4))
+        permp = ctx.enter_context(tc.tile_pool(name="permp", bufs=2))
         psum = ctx.enter_context(tc.psum_pool(name="psum", bufs=8))
         ctx.enter_context(tc.manual_schedule())
 
@@ -107,10 +108,11 @@ def tile_selfattention_pb_t_kernel(tc, attn, tokens, Wv, bv, out):
             else:
                 nc.vector.tensor_copy(out=dst, in_=src)
 
-        def transposes(key, words, offs):
+        def transposes(key, words, offs, step=2):
             bank = new_bank()
             for n, off in enumerate(offs):
-                nc.tensor.transpose(bank[:, n * P : (n + 1) * P], words[:, off : off + 2 * P - 1 : 2], ident[:])
+                stop = off + step * (P - 1) + 1
+                nc.tensor.transpose(bank[:, n * P : (n + 1) * P], words[:, off:stop:step], ident[:])
             live[key] = bank
 
         def evac_words(key, grp, half, eng):
@@ -181,14 +183,28 @@ def tile_selfattention_pb_t_kernel(tc, attn, tokens, Wv, bv, out):
                 for g in (0, 1):
                     live[("ag", i, g)] = sgrp.tile([P, 2048], BF16, name="grp_s", tag="s", align_bytes=64)
             for j in halves:
-                words = at_raw[(i, j)][:].bitcast(F32)
+                sorted_words = live.get(("ap", i, j))
+                if sorted_words is None:
+                    words, step, piece, apart = at_raw[(i, j)][:].bitcast(F32), 2, 256, 1
+                else:
+                    words, step, piece, apart = sorted_words[:].bitcast(F32), 1, P, 512
                 for g in (0, 1):
                     transposes(
                         ("at", i, g, j),
                         words,
-                        [b * 512 + g * 256 + u for b in (0, 1) for u in (0, 1)],
+                        [(2 * b + g) * piece + u * apart for b in (0, 1) for u in (0, 1)],
+                        step,
                     )
                     evac_words(("at", i, g, j), live[("ag", i, g)], j, "s")
+
+        def ap(i, j, eng):
+            sorted_words = permp.tile([P, 2048], BF16, name="sorted_words", tag="sw")
+            copy_out(
+                eng,
+                sorted_words[:].bitcast(F32).rearrange("l (u y) -> l y u", u=2),
+                at_raw[(i, j)][:].bitcast(F32).rearrange("l (y u) -> l y u", u=2),
+            )
+            live[("ap", i, j)] = sorted_words
 
         def aq(i, g):
             quantise(at_cs[(i, g)], live[("ag", i, g)])
@@ -254,6 +270,8 @@ def tile_selfattention_pb_t_kernel(tc, attn, tokens, Wv, bv, out):
             if s in (4, 5):
                 wq(1, s - 4)
             split = s in (0, 2, 3)
+            if s % 2 == 1 and s < 10:
+                ap((s + 6) // 2, (s + 6) % 2, "v")
             for j in (2 * s, 2 * s + 1):
                 n = j + LEAD
                 if s % 2 == 1 and (s + 3) // 2 < 8:

from contextlib import ExitStack

import concourse.mybir as mybir
from concourse.masks import make_identity

F32 = mybir.dt.float32
BF16 = mybir.dt.bfloat16
U32 = mybir.dt.uint32
U8 = mybir.dt.uint8
FP8X4 = mybir.dt.float8_e4m3fn_x4
ADD = mybir.AluOpType.add

P = 128
FLOPS = 2 * 2048 * 1024 * 512 + 2 * 4 * 512 * 1024 * 1024

LEAD = 4
FIRST_LOADS = 5


def tile_selfattention_pb_t_kernel(tc, attn, tokens, Wv, bv, out):
    nc = tc.nc
    with ExitStack() as ctx:
        const = ctx.enter_context(tc.tile_pool(name="const", bufs=1))
        raw = ctx.enter_context(tc.tile_pool(name="raw", bufs=1))
        codes = ctx.enter_context(tc.tile_pool(name="codes", bufs=1))
        sgrp = ctx.enter_context(tc.tile_pool(name="sgrp", bufs=5))
        wgrp = ctx.enter_context(tc.tile_pool(name="wgrp", bufs=4))
        tgrp = ctx.enter_context(tc.tile_pool(name="tgrp", bufs=2))
        vgrp = ctx.enter_context(tc.tile_pool(name="vgrp", bufs=4))
        outp = ctx.enter_context(tc.tile_pool(name="outp", bufs=4))
        permp = ctx.enter_context(tc.tile_pool(name="permp", bufs=2))
        psum = ctx.enter_context(tc.psum_pool(name="psum", bufs=8))
        ctx.enter_context(tc.manual_schedule())

        wv_view = Wv.rearrange("(g q u e a) k -> g u a q e k", g=2, u=2, e=2, a=2)
        tok_view = tokens.rearrange("(q t) c -> q t c", t=4)
        wv_raw = {
            (a, gu): raw.tile([P, 2, 512], BF16, name="wv_raw%d%d" % (a, gu)) for a in range(2) for gu in range(4)
        }
        tok_raw = [raw.tile([P, 4, 512], BF16, name="tok_raw%d" % cb) for cb in range(2)]
        at_raw = {(i, j): raw.tile([P, 2048], BF16, name="at_raw%d%d" % (i, j)) for i in range(8) for j in range(2)}
        bias_raw = const.tile([P, 2, 4, 2], BF16, name="bias_raw")
        bias_f = const.tile([P, 2, 8], F32, name="bias_f")
        ident = const.tile([P, P], F32, name="ident")

        def load_attn(i):
            h, lh = divmod(i, 2)
            view = attn[h, lh * 512 : (lh + 1) * 512, :].rearrange("(lp j b) m -> j lp (b m)", j=2, b=2)
            for j in (0, 1):
                nc.sync.dma_start(out=at_raw[(i, j)][:], in_=view[j])

        def load_wv(a, g):
            for u in (0, 1):
                nc.sync.dma_start(out=wv_raw[(a, 2 * g + u)][:], in_=wv_view[g, u, a])

        with nc.allow_non_contiguous_dma(reason="bias: 8-byte runs, 4 KiB in all"):
            nc.scalar.dma_start(
                out=bias_raw[:], in_=bv.rearrange("(g q t a) -> q g t a", g=2, t=4, a=2)
            )
        make_identity(nc, ident[:])
        def load_tokens(cb):
            for u in (0, 1):
                nc.sync.dma_start(
                    out=tok_raw[cb][:, 2 * u : 2 * u + 2, :],
                    in_=tok_view[:, 2 * u : 2 * u + 2, cb * 512 : (cb + 1) * 512],
                )

        load_wv(0, 0)
        load_tokens(0)
        load_wv(0, 1)
        load_attn(0)
        load_attn(1)
        load_attn(2)
        load_tokens(1)
        load_attn(3)
        load_wv(1, 0)
        load_wv(1, 1)
        for i in range(4, FIRST_LOADS):
            load_attn(i)

        def code_pair(name, width):
            c = codes.tile([P, width], U32, name=name + "_c", align_bytes=64)
            s = codes.tile([P, width], U8, name=name + "_s", align_bytes=64)
            return c, s

        tok_cs = [code_pair("tok%d" % cb, 512) for cb in range(2)]
        wv_cs = {(a, g): code_pair("wv%d%d" % (a, g), 512) for a in range(2) for g in range(2)}
        at_cs = {(i, g): code_pair("at%d%d" % (i, g), 512) for i in range(8) for g in range(2)}
        v_cs = {
            (h, g, k): code_pair("v%d%d%d" % (h, g, k), P)
            for h in range(4)
            for g in range(2)
            for k in range(4)
        }

        def quantise(pair, grp):
            nc.vector.quantize_mx(out=pair[0][:].bitcast(FP8X4), scales=pair[1][:], in_=grp[:])

        live = {"waiting": None}

        def new_bank():
            bank = psum.tile([P, 512], F32, name="bank", tag="bank")
            return bank

        def copy_out(eng, dst, src):
            if eng == "s":
                nc.scalar.copy(out=dst, in_=src)
            else:
                nc.vector.tensor_copy(out=dst, in_=src)

        def transposes(key, words, offs, step=2):
            bank = new_bank()
            for n, off in enumerate(offs):
                stop = off + step * (P - 1) + 1
                nc.tensor.transpose(bank[:, n * P : (n + 1) * P], words[:, off:stop:step], ident[:])
            live[key] = bank

        def evac_words(key, grp, half, eng):
            dst = grp[:].bitcast(F32)[:, half * 512 : (half + 1) * 512].rearrange(
                "p (b c k) -> p b c k", b=2, k=2
            )
            copy_out(eng, dst, live[key][:].rearrange("p (b k c) -> p b c k", b=2, k=2))

        def wt(a, g, u, eng="s"):
            words = wv_raw[(a, 2 * g + u)][:].rearrange("q e k -> q (e k)").bitcast(F32)
            transposes(("wt", a, g, u), words, [e * 256 + uk for e in (0, 1) for uk in (0, 1)])
            if u == 0:
                live[("wg", a, g)] = wgrp.tile([P, 2048], BF16, name="grp_w", tag="w", align_bytes=64)
            evac_words(("wt", a, g, u), live[("wg", a, g)], u, eng)

        def wq(a, g):
            quantise(wv_cs[(a, g)], live[("wg", a, g)])

        def tk_r(cb, eng):
            tg = tgrp.tile([P, 2048], BF16, name="grp_t", tag="t", align_bytes=64)
            copy_out(
                eng,
                tg[:].rearrange("p (c i t) -> p c t i", i=4, t=4),
                tok_raw[cb][:].rearrange("p t (c i) -> p c t i", i=4),
            )
            live[("tg", cb)] = tg

        def tk_q(cb):
            quantise(tok_cs[cb], live[("tg", cb)])

        def m1(n):
            h, k, g = n // 8, (n // 2) % 4, n % 2
            a, cb = divmod(h, 2)
            bank = new_bank()
            wc, ws = wv_cs[(a, g)]
            tcd, tsc = tok_cs[cb]
            for t in range(4):
                nc.tensor.matmul_mx(
                    out=bank[:, t * P : (t + 1) * P],
                    lhsT=wc[:, t * P : (t + 1) * P].bitcast(FP8X4),
                    lhsT_scale=ws[:, t * P : (t + 1) * P],
                    rhs=tcd[:, k * P : (k + 1) * P].bitcast(FP8X4),
                    rhs_scale=tsc[:, k * P : (k + 1) * P],
                    start=True,
                    stop=True,
                )
            live[("vb", n)] = bank

        def ve(n):
            h, k, g = n // 8, (n // 2) % 4, n % 2
            vg = vgrp.tile([P, 512], BF16, name="grp_v", tag="v", align_bytes=64)
            nc.vector.tensor_tensor(
                out=vg[:].rearrange("q (d t) -> q d t", t=4),
                in0=live[("vb", n)][:].rearrange("q (t d) -> q d t", t=4),
                in1=bias_f[:, h // 2, 4 * g : 4 * g + 4].unsqueeze(1).to_broadcast([P, P, 4]),
                op=ADD,
            )
            vq_flush()
            live["waiting"] = (v_cs[(h, g, k)], vg)

        def vq_flush():
            if live["waiting"] is not None:
                quantise(live["waiting"][0], live["waiting"][1])
            live["waiting"] = None

        def at(i, halves=(0, 1)):
            if 0 in halves:
                for g in (0, 1):
                    live[("ag", i, g)] = sgrp.tile([P, 2048], BF16, name="grp_s", tag="s", align_bytes=64)
            for j in halves:
                sorted_words = live.get(("ap", i, j))
                if sorted_words is None:
                    words, step, piece, apart = at_raw[(i, j)][:].bitcast(F32), 2, 256, 1
                else:
                    words, step, piece, apart = sorted_words[:].bitcast(F32), 1, P, 512
                for g in (0, 1):
                    transposes(
                        ("at", i, g, j),
                        words,
                        [(2 * b + g) * piece + u * apart for b in (0, 1) for u in (0, 1)],
                        step,
                    )
                    evac_words(("at", i, g, j), live[("ag", i, g)], j, "s")

        def ap(i, j, eng):
            sorted_words = permp.tile([P, 2048], BF16, name="sorted_words", tag="sw")
            copy_out(
                eng,
                sorted_words[:].bitcast(F32).rearrange("l (u y) -> l y u", u=2),
                at_raw[(i, j)][:].bitcast(F32).rearrange("l (y u) -> l y u", u=2),
            )
            live[("ap", i, j)] = sorted_words

        def aq(i, g):
            quantise(at_cs[(i, g)], live[("ag", i, g)])

        def m2(j, eng):
            h, k, lh = j // 8, (j // 2) % 4, j % 2
            bank = new_bank()
            for g in (0, 1):
                vc, vs = v_cs[(h, g, k)]
                ac, asc = at_cs[(2 * h + lh, g)]
                nc.tensor.matmul_mx(
                    out=bank[:],
                    lhsT=vc[:].bitcast(FP8X4),
                    lhsT_scale=vs[:],
                    rhs=ac[:].bitcast(FP8X4),
                    rhs_scale=asc[:],
                    start=(g == 0),
                    stop=(g == 1),
                )
            if lh == 0:
                live["osb"] = outp.tile([P, 1024], F32, name="out_sb", tag="o")
            osb = live["osb"]
            copy_out(
                eng,
                osb[:, lh * 512 : (lh + 1) * 512].rearrange("d (lp lb) -> d lp lb", lb=4),
                bank[:].rearrange("d (lb lp) -> d lp lb", lb=4),
            )
            if j >= 30:
                l0 = lh * 512
                nc.sync.dma_start(out=out[h, k * P : (k + 1) * P, l0 : l0 + 512], in_=osb[:, l0 : l0 + 512])
            elif lh == 1:
                nc.sync.dma_start(out=out[h, k * P : (k + 1) * P, :], in_=osb[:])

        for g in (0, 1):
            for u in (0, 1):
                wt(0, g, u)
        tk_r(0, "v")
        wq(0, 0)
        tk_q(0)
        wq(0, 1)
        for a in (0, 1):
            nc.vector.tensor_copy(
                out=bias_f[:, a, :].rearrange("q (g t) -> q g t", t=4), in_=bias_raw[:, :, :, a]
            )
        at(0, (0,))
        for n in range(LEAD):
            m1(n)
            ve(n)
        at(0, (1,))
        aq(0, 0)
        aq(0, 1)
        at(1)
        aq(1, 0)
        aq(1, 1)
        for s in range(16):
            early = 4 if s == 0 else s + 5
            if early < 16:
                at(early // 2, (early % 2,))
            if s == 0:
                tk_r(1, "v")
            if s == 1:
                tk_q(1)
            if s in (4, 5):
                wq(1, s - 4)
            split = s in (0, 2, 3)
            if s % 2 == 1 and s < 10:
                ap((s + 6) // 2, (s + 6) % 2, "v")
            for j in (2 * s, 2 * s + 1):
                n = j + LEAD
                if s % 2 == 1 and (s + 3) // 2 < 8:
                    aq((s + 3) // 2, j % 2)
                if split and j % 2 == 1:
                    m2(j - 1, "s")
                    if s == 0:
                        at(2, (1,))
                    else:
                        for u in (0, 1):
                            wt(1, s - 2, u)
                if n < 32:
                    m1(n)
                    ve(n)
                if n == 31:
                    vq_flush()
            for j in ((2 * s + 1,) if split else (2 * s, 2 * s + 1)):
                m2(j, "v" if (j + LEAD >= 32 and j % 2 == 1) else "s")
            if s % 2 == 1 and s // 2 + FIRST_LOADS < 8:
                load_attn(s // 2 + FIRST_LOADS)
